import numpy as np
import ml_dtypes


def mxq(x, axis, fmt="e4m3"):
    dtype, down = {"e4m3": (ml_dtypes.float8_e4m3fn, 7), "e5m2": (ml_dtypes.float8_e5m2, 14)}[fmt]
    v = np.moveaxis(np.asarray(x, np.float32).astype(ml_dtypes.bfloat16).astype(np.float64), axis, -1)
    blocks = v.reshape(v.shape[:-1] + (-1, 32))
    amax = np.abs(blocks).max(-1, keepdims=True)
    byte = np.maximum(np.where(amax > 0, np.frexp(amax)[1] - 1 + 127, 0) - down, 1)
    scale = np.exp2(byte - 127.0)
    codes = (blocks / scale).astype(np.float32).astype(dtype).astype(np.float64)
    return np.moveaxis((codes * scale).reshape(v.shape), -1, axis)


WIDE = False


def mx_kscale(k):
    if not WIDE:
        return np.ones(k)
    levels = np.array([10, -10, 5, -5, 0])
    if k % 512:
        return np.exp2(np.random.permutation(np.resize(levels, k // 32))).repeat(32)
    a = np.empty((k // 512, 16))
    for p in range(k // 512):
        a[p, :8] = np.random.permutation(np.resize(levels, 8))
        for g in range(8):
            far = levels[np.abs(levels - a[p, g]) >= 10]
            a[p, g + 8] = far[np.random.randint(len(far))]
    return np.exp2(a.ravel()).repeat(32)


BF16 = ml_dtypes.bfloat16


def bf(x):
    return np.asarray(x, np.float32).astype(BF16)


def f64(x):
    return np.asarray(x).astype(np.float64)


B, T, D, H, DH = 2, 256, 2048, 16, 128
E = H * DH
EPS = 1e-6
ROPE_BASE = 10000.0


def rms_norm(t):
    return t / np.sqrt(np.mean(t * t, axis=-1, keepdims=True) + EPS)


def rope(t):
    inv_freq = 1.0 / ROPE_BASE ** (np.arange(0, DH, 2) / DH)
    ang = np.arange(T)[:, None] * inv_freq[None, :]
    cos, sin = np.cos(ang), np.sin(ang)
    t1, t2 = t[..., :DH // 2], t[..., DH // 2:]
    return np.concatenate([t1 * cos - t2 * sin, t1 * sin + t2 * cos], axis=-1)


def draw0():
    s = mx_kscale(D)
    return {"x": bf(np.random.standard_normal((B, T, D)) * s),
            "W_qk": bf(np.random.standard_normal((D, 2 * E)) / np.sqrt(D) / s[:, None])}


def core(x, W_qk):
    qk = mxq(f64(x), 2, "e4m3") @ mxq(f64(W_qk), 0, "e4m3")
    qk = qk.reshape(B, T, 2, H, DH).transpose(2, 0, 3, 1, 4)
    q, k = rms_norm(qk[0]), rms_norm(qk[1])
    return rope(q), rope(k)


def e4m3fn_bytes(y):
    return np.clip(np.asarray(y, np.float64), -448.0, 448.0).astype(np.float32).astype(ml_dtypes.float8_e4m3fn).view(np.uint8)


def e4m3fn_values(b):
    return np.asarray(b, np.uint8).view(ml_dtypes.float8_e4m3fn).astype(np.float64)


def setup_inputs():
    d = draw0()
    x0 = np.asarray(d['W_qk']).astype(np.float64)
    s = (np.max(np.abs(x0), axis=(1,), keepdims=True) / 448.0).astype(np.float32)
    out = {}
    for k, v in d.items():
        if k == 'W_qk':
            out['W_qk_bytes'] = e4m3fn_bytes(x0 / s.astype(np.float64))
            out['W_qk_scale'] = s
        else:
            out[k] = v
    return out


def reference(x, W_qk_bytes, W_qk_scale):
    return core(x, e4m3fn_values(W_qk_bytes) * W_qk_scale.astype(np.float64))

@@ -1,0 +1,254 @@
+from contextlib import ExitStack
+import math
+
+import concourse.mybir as mybir
+from concourse.masks import make_identity
+
+F32 = mybir.dt.float32
+BF16 = mybir.dt.bfloat16
+U32 = mybir.dt.uint32
+U8 = mybir.dt.uint8
+I32 = mybir.dt.int32
+FP8 = mybir.dt.float8_e4m3fn
+FP8X4 = mybir.dt.float8_e4m3fn_x4
+ALU = mybir.AluOpType
+ACT = mybir.ActivationFunctionType
+
+B, T, D, H, DH = 2, 256, 2048, 16, 128
+E = H * DH
+EPS = 1e-6
+ROPE_BASE = 10000.0
+FLOPS = 2 * B * T * D * 2 * E
+
+P = 128
+PACK = 4
+K_PASS = P * PACK
+PASSES = D // K_PASS
+N_TILE = 512
+CHUNKS = 2 * E // N_TILE
+HEADS_PER_CHUNK = N_TILE // DH
+M_TILES = B * T // P
+HALF = DH // 2
+STEPS = CHUNKS * PASSES
+EPI_LAG = 5
+
+def vector_planes(s):
+    if s < 4:
+        return 2
+    return 0
+
+
+def tile_attn_pa_kernel(tc, x, W_qk_bytes, W_qk_scale, out_0, out_1):
+    nc = tc.nc
+    outs = (out_0, out_1)
+    xf = x.flatten_outer_dims()
+    wv = W_qk_bytes.rearrange("(g p t) n -> g p t n", p=P, t=PACK)
+
+    with ExitStack() as ctx:
+        const = ctx.enter_context(tc.tile_pool(name="const", bufs=1))
+        xpool = ctx.enter_context(tc.tile_pool(name="xpool", bufs=1))
+        wbytes = ctx.enter_context(tc.tile_pool(name="wbytes", bufs=STEPS))
+        wprep = ctx.enter_context(tc.tile_pool(name="wprep", bufs=3))
+        wq = ctx.enter_context(tc.tile_pool(name="wq", bufs=12))
+        epi = ctx.enter_context(tc.tile_pool(name="epi", bufs=4))
+        small = ctx.enter_context(tc.tile_pool(name="small", bufs=6))
+        psum = ctx.enter_context(tc.psum_pool(name="psum", bufs=8))
+
+        sc = const.tile([P, PASSES * PACK], F32, name="sc")
+        nc.scalar.dma_start(
+            out=sc[:].rearrange("p (g t) -> p g t", t=PACK),
+            in_=W_qk_scale.rearrange("(g p t) o -> p g (t o)", p=P, t=PACK),
+        )
+        wb = []
+        xs = []
+
+        def load_w(s):
+            c, g = divmod(s, PASSES)
+            w_codes_in = wbytes.tile([P, PACK, N_TILE], U8, name="w_codes_in")
+            nc.sync.dma_start(out=w_codes_in[:], in_=wv[g][:, :, c * N_TILE:(c + 1) * N_TILE])
+            wb.append(w_codes_in)
+
+        for s in range(PASSES):
+            load_w(s)
+        for m in range(M_TILES):
+            x_rows = xpool.tile([P, D], BF16, name="x_rows%d" % m)
+            nc.sync.dma_start(out=x_rows[:], in_=xf[m * P:(m + 1) * P, :])
+            xs.append(x_rows)
+        for s in range(PASSES, STEPS):
+            load_w(s)
+
+        ident = const.tile([P, P], F32, name="ident")
+        make_identity(nc, ident[:])
+        pos_i = const.tile([P, 2], I32, name="pos_i")
+        nc.gpsimd.iota(pos_i[:], pattern=[[P, 2]], base=0, channel_multiplier=1)
+        pos = const.tile([P, 2], F32, name="pos")
+        nc.vector.tensor_copy(out=pos[:], in_=pos_i[:])
+        tau = const.tile([P, HALF], F32, name="tau")
+        nc.vector.memset(tau[:, 0:1], 1.0)
+        nc.vector.tensor_scalar(out=tau[:, 0:1], in0=tau[:, 0:1], scalar1=1.0 / (2.0 * math.pi),
+                                scalar2=None, op0=ALU.mult)
+        ratio = ROPE_BASE ** (-1.0 / HALF)
+        n = 1
+        while n < HALF:
+            nc.vector.tensor_scalar(out=tau[:, n:2 * n], in0=tau[:, 0:n], scalar1=ratio ** n,
+                                    scalar2=None, op0=ALU.mult)
+            n *= 2
+        turns = const.tile([P, 2, 2, HALF], F32, name="turns")
+        for a in range(2):
+            nc.vector.tensor_scalar(out=turns[:, a, 0, :], in0=tau[:], scalar1=pos[:, a:a + 1],
+                                    scalar2=None, op0=ALU.mult)
+            nc.vector.tensor_scalar(out=turns[:, a, 1, :], in0=tau[:], scalar1=pos[:, a:a + 1],
+                                    scalar2=0.25, op0=ALU.mult, op1=ALU.add)
+        whole_i = const.tile([P, 2, 2, HALF], I32, name="whole_i")
+        nc.vector.tensor_copy(out=whole_i[:], in_=turns[:])
+        whole = const.tile([P, 2, 2, HALF], F32, name="whole")
+        nc.vector.tensor_copy(out=whole[:], in_=whole_i[:])
+        frac = const.tile([P, 2, 2, HALF], F32, name="frac")
+        nc.vector.tensor_tensor(out=frac[:], in0=turns[:], in1=whole[:], op=ALU.subtract)
+        over = const.tile([P, 2, 2, HALF], F32, name="over")
+        nc.vector.tensor_scalar(out=over[:], in0=frac[:], scalar1=0.5, scalar2=None, op0=ALU.is_gt)
+        nc.vector.tensor_tensor(out=frac[:], in0=frac[:], in1=over[:], op=ALU.subtract)
+        trig = const.tile([P, 2, 3, HALF], F32, name="trig")
+        nc.scalar.activation(out=trig[:, :, 0, :], in_=frac[:, :, 0, :], func=ACT.Sin, scale=2.0 * math.pi)
+        nc.scalar.activation(out=trig[:, :, 1, :], in_=frac[:, :, 0, :], func=ACT.Sin, scale=-2.0 * math.pi)
+        nc.scalar.activation(out=trig[:, :, 2, :], in_=frac[:, :, 1, :], func=ACT.Sin, scale=2.0 * math.pi)
+        eps_col = const.tile([P, 1], F32, name="eps_col")
+        nc.vector.memset(eps_col[:], EPS)
+        warm = const.tile([P, 1], F32, name="warm")
+        nc.scalar.activation(out=warm[:], in_=tau[:, 0:1], func=ACT.Abs_reciprocal_sqrt, bias=eps_col[:, 0:1])
+
+        x_codes = []
+        x_scales = []
+
+        def prep_x(m):
+            words = xs[m][:].bitcast(F32)
+            x_grouped = xpool.tile([P, PASSES * P * PACK], BF16, name="x_grouped%d" % m, align_bytes=64)
+            gw = x_grouped[:].bitcast(F32).rearrange("p (g r u) -> p g r u", g=PASSES, u=2)
+            for gp in range(PASSES // 2):
+                xt = psum.tile([P, 2, 2, P], F32, name="xt", tag="bank")
+                for gi in range(2):
+                    g = 2 * gp + gi
+                    for u in range(2):
+                        nc.tensor.transpose(xt[:, gi, u, :], words[:, 256 * g + u:256 * (g + 1):2], ident[:])
+                src = xt[:].rearrange("p g u r -> p g r u")
+                dst = gw[:, 2 * gp:2 * gp + 2, :, :]
+                if gp == 0:
+                    nc.vector.tensor_copy(out=dst, in_=src)
+                else:
+                    nc.scalar.copy(out=dst, in_=src)
+            xc = xpool.tile([P, PASSES * P], U32, name="x_codes%d" % m, align_bytes=64)
+            xsc = xpool.tile([P, PASSES * P], U8, name="x_scales%d" % m, align_bytes=64)
+            nc.vector.quantize_mx(out=xc[:].bitcast(FP8X4), scales=xsc[:], in_=x_grouped[:])
+            x_codes.append(xc)
+            x_scales.append(xsc)
+
+        planes = {}
+        grouped = {}
+        w_codes = {}
+        w_scales = {}
+        acc = {}
+
+        def widen(s):
+            g = s % PASSES
+            pl = wprep.tile([P, PACK, N_TILE], BF16, name="pl", bufs=4)
+            nv = vector_planes(s)
+            for t in range(PACK):
+                col = sc[:, g * PACK + t:g * PACK + t + 1]
+                src = wb[s][:, t, :].bitcast(FP8)
+                if t < nv:
+                    nc.vector.tensor_scalar(out=pl[:, t, :], in0=src, scalar1=col, scalar2=None, op0=ALU.mult)
+                else:
+                    nc.scalar.activation(out=pl[:, t, :], in_=src, func=ACT.Copy, scale=col)
+            planes[s] = pl
+
+        def interleave(s):
+            il = wprep.tile([P, N_TILE, PACK], BF16, name="il", align_bytes=64)
+            nc.vector.tensor_copy(out=il[:].rearrange("p (c i) t -> p c t i", i=4),
+                                  in_=planes[s][:].rearrange("p t (c i) -> p c t i", i=4))
+            grouped[s] = il
+
+        def quantize(s):
+            wc = wq.tile([P, N_TILE], U32, name="wc", align_bytes=64)
+            ws = wq.tile([P, N_TILE], U8, name="ws", align_bytes=64)
+            nc.vector.quantize_mx(out=wc[:].bitcast(FP8X4), scales=ws[:],
+                                  in_=grouped[s][:].rearrange("p n t -> p (n t)"))
+            w_codes[s] = wc
+            w_scales[s] = ws
+
+        def multiply(s):
+            c, g = divmod(s, PASSES)
+            for m in range(M_TILES):
+                if g == 0:
+                    bank = psum.tile([P, N_TILE], F32, name="acc", tag="bank")
+                    acc[(c, m)] = bank
+                cols = slice(g * P, (g + 1) * P)
+                nc.tensor.matmul_mx(
+                    out=acc[(c, m)][:],
+                    lhsT=x_codes[m][:, cols].bitcast(FP8X4), lhsT_scale=x_scales[m][:, cols],
+                    rhs=w_codes[s][:].bitcast(FP8X4), rhs_scale=w_scales[s][:],
+                    start=(g == 0), stop=(g == PASSES - 1),
+                )
+
+        rot = {}
+
+        def epi_rotate(e):
+            c, m = divmod(e, M_TILES)
+            a = m % 2
+            bank = acc[(c, m)]
+            ta = epi.tile([P, HEADS_PER_CHUNK, 2, HALF], F32, name="ta", bufs=6)
+            tb = epi.tile([P, HEADS_PER_CHUNK, 2, HALF], F32, name="tb", bufs=3)
+            bv = bank[:].rearrange("p (h w i) -> p h w i", w=2, i=HALF)
+            shape = [P, HEADS_PER_CHUNK, 2, HALF]
+            nc.vector.tensor_tensor(out=ta[:], in0=bv,
+                                    in1=trig[:, a, 2:3, :].unsqueeze(1).to_broadcast(shape), op=ALU.mult)
+            nc.vector.tensor_tensor(out=tb[:], in0=bv,
+                                    in1=trig[:, a, 0:2, :].unsqueeze(1).to_broadcast(shape), op=ALU.mult)
+            rot[e] = (ta, tb)
+
+        def epi_add(e):
+            ta, tb = rot[e]
+            nc.vector.tensor_tensor(out=ta[:], in0=ta[:], in1=tb[:, :, ::-1, :], op=ALU.add)
+
+        def epi_scale_store(e):
+            c, m = divmod(e, M_TILES)
+            ta, tb = rot[e]
+            ss = small.tile([P, HEADS_PER_CHUNK], F32, name="ss")
+            for h in range(HEADS_PER_CHUNK):
+                junk = small.tile([P, DH], F32, name="junk", bufs=2)
+                nc.scalar.activation(out=junk[:].rearrange("p (w i) -> p w i", w=2), in_=ta[:, h, :, :],
+                                     func=ACT.Square, accum_out=ss[:, h:h + 1])
+            r = small.tile([P, HEADS_PER_CHUNK], F32, name="r")
+            nc.scalar.activation(out=r[:], in_=ss[:], func=ACT.Abs_reciprocal_sqrt, scale=1.0 / DH,
+                                 bias=eps_col[:, 0:1])
+            for h in range(HEADS_PER_CHUNK):
+                nc.scalar.activation(out=ta[:, h, :, :], in_=ta[:, h, :, :], func=ACT.Copy, scale=r[:, h:h + 1])
+            dst = outs[c // (CHUNKS // 2)]
+            h0 = (c % (CHUNKS // 2)) * HEADS_PER_CHUNK
+            b, a = divmod(m, 2)
+            nc.sync.dma_start(
+                out=dst[b, h0:h0 + HEADS_PER_CHUNK, a * P:(a + 1) * P, :].rearrange("h t d -> t h d"),
+                in_=ta[:].rearrange("p h w i -> p h (w i)"))
+
+        widen(0)
+        widen(1)
+        for i in range(STEPS + EPI_LAG + 1):
+            e = i - EPI_LAG
+            if 0 <= e - 1 < STEPS:
+                epi_scale_store(e - 1)
+            if i + 2 < STEPS:
+                widen(i + 2)
+            if i < STEPS:
+                interleave(i)
+            if i < M_TILES:
+                prep_x(i)
+            if 0 <= e < STEPS:
+                epi_rotate(e)
+            if i < STEPS:
+                quantize(i)
+            if i == M_TILES - 1:
+                for s in range(M_TILES):
+                    multiply(s)
+            elif M_TILES <= i < STEPS:
+                multiply(i)
+            if 0 <= e < STEPS:
+                epi_add(e)

@@ -32,16 +32,27 @@ HALF = DH // 2
 STEPS = CHUNKS * PASSES
 EPI_LAG = 5
 
+TOK = B * T
+HEADS = 2 * H
+LAG_MX = 4
+LAG_ROT = 5
+LAG_NORM = 6
+
+
 def vector_planes(s):
     if s < 4:
         return 2
     return 0
 
 
+def vector_scales(hd):
+    return hd % 2 == 1
+
+
 def tile_attn_pa_kernel(tc, x, W_qk_bytes, W_qk_scale, out_0, out_1):
     nc = tc.nc
     outs = (out_0, out_1)
-    xf = x.flatten_outer_dims()
+    xv = x.flatten_outer_dims().rearrange("(m p) k -> p m k", p=P)
     wv = W_qk_bytes.rearrange("(g p t) n -> g p t n", p=P, t=PACK)
 
     with ExitStack() as ctx:
@@ -50,9 +61,9 @@ def tile_attn_pa_kernel(tc, x, W_qk_bytes, W_qk_scale, out_0, out_1):
         wbytes = ctx.enter_context(tc.tile_pool(name="wbytes", bufs=STEPS))
         wprep = ctx.enter_context(tc.tile_pool(name="wprep", bufs=3))
         wq = ctx.enter_context(tc.tile_pool(name="wq", bufs=12))
-        epi = ctx.enter_context(tc.tile_pool(name="epi", bufs=4))
+        epi = ctx.enter_context(tc.tile_pool(name="epi", bufs=3))
         small = ctx.enter_context(tc.tile_pool(name="small", bufs=6))
-        psum = ctx.enter_context(tc.psum_pool(name="psum", bufs=8))
+        psum = ctx.enter_context(tc.psum_pool(name="psum", bufs=4))
 
         sc = const.tile([P, PASSES * PACK], F32, name="sc")
         nc.scalar.dma_start(
@@ -68,17 +79,25 @@ def tile_attn_pa_kernel(tc, x, W_qk_bytes, W_qk_scale, out_0, out_1):
             nc.sync.dma_start(out=w_codes_in[:], in_=wv[g][:, :, c * N_TILE:(c + 1) * N_TILE])
             wb.append(w_codes_in)
 
-        for s in range(PASSES):
-            load_w(s)
-        for m in range(M_TILES):
-            x_rows = xpool.tile([P, D], BF16, name="x_rows%d" % m)
-            nc.sync.dma_start(out=x_rows[:], in_=xf[m * P:(m + 1) * P, :])
+        def load_x(g):
+            x_rows = xpool.tile([P, M_TILES, K_PASS], BF16, name="x_rows%d" % g)
+            nc.sync.dma_start(out=x_rows[:], in_=xv[:, :, g * K_PASS:(g + 1) * K_PASS])
             xs.append(x_rows)
+
+        load_w(0)
+        load_w(1)
+        for g in range(PASSES):
+            load_x(g)
+            if g + 2 < PASSES:
+                load_w(g + 2)
         for s in range(PASSES, STEPS):
             load_w(s)
 
         ident = const.tile([P, P], F32, name="ident")
         make_identity(nc, ident[:])
+        swp = const.tile([P, P], F32, name="swp")
+        nc.vector.tensor_copy(out=swp[:, 0:HALF], in_=ident[:, HALF:P])
+        nc.vector.tensor_copy(out=swp[:, HALF:P], in_=ident[:, 0:HALF])
         pos_i = const.tile([P, 2], I32, name="pos_i")
         nc.gpsimd.iota(pos_i[:], pattern=[[P, 2]], base=0, channel_multiplier=1)
         pos = const.tile([P, 2], F32, name="pos")
@@ -108,36 +127,43 @@ def tile_attn_pa_kernel(tc, x, W_qk_bytes, W_qk_scale, out_0, out_1):
         over = const.tile([P, 2, 2, HALF], F32, name="over")
         nc.vector.tensor_scalar(out=over[:], in0=frac[:], scalar1=0.5, scalar2=None, op0=ALU.is_gt)
         nc.vector.tensor_tensor(out=frac[:], in0=frac[:], in1=over[:], op=ALU.subtract)
-        trig = const.tile([P, 2, 3, HALF], F32, name="trig")
+        trig = const.tile([P, 2, 4, HALF], F32, name="trig")
         nc.scalar.activation(out=trig[:, :, 0, :], in_=frac[:, :, 0, :], func=ACT.Sin, scale=2.0 * math.pi)
         nc.scalar.activation(out=trig[:, :, 1, :], in_=frac[:, :, 0, :], func=ACT.Sin, scale=-2.0 * math.pi)
         nc.scalar.activation(out=trig[:, :, 2, :], in_=frac[:, :, 1, :], func=ACT.Sin, scale=2.0 * math.pi)
+        nc.scalar.activation(out=trig[:, :, 3, :], in_=frac[:, :, 1, :], func=ACT.Sin, scale=2.0 * math.pi)
         eps_col = const.tile([P, 1], F32, name="eps_col")
         nc.vector.memset(eps_col[:], EPS)
         warm = const.tile([P, 1], F32, name="warm")
         nc.scalar.activation(out=warm[:], in_=tau[:, 0:1], func=ACT.Abs_reciprocal_sqrt, bias=eps_col[:, 0:1])
+        tab_ps = psum.tile([P, 2, 2, P], F32, name="tab_ps", tag="tr")
+        for k in range(2):
+            for a in range(2):
+                nc.tensor.transpose(tab_ps[:, k, a, :],
+                                    trig[:, a, 2 * k:2 * k + 2, :].rearrange("p w i -> p (w i)"), ident[:])
+        tab = const.tile([P, 2, T], F32, name="tab")
+        nc.vector.tensor_copy(out=tab[:].rearrange("p k (a t) -> p k a t", a=2), in_=tab_ps[:])
 
         x_codes = []
         x_scales = []
 
-        def prep_x(m):
-            words = xs[m][:].bitcast(F32)
-            x_grouped = xpool.tile([P, PASSES * P * PACK], BF16, name="x_grouped%d" % m, align_bytes=64)
-            gw = x_grouped[:].bitcast(F32).rearrange("p (g r u) -> p g r u", g=PASSES, u=2)
-            for gp in range(PASSES // 2):
-                xt = psum.tile([P, 2, 2, P], F32, name="xt", tag="bank")
-                for gi in range(2):
-                    g = 2 * gp + gi
+        def prep_x(g):
+            words = xs[g][:].bitcast(F32)
+            x_grouped = xpool.tile([P, TOK * PACK], BF16, name="x_grouped%d" % g, align_bytes=64)
+            gw = x_grouped[:].bitcast(F32).rearrange("p (m r u) -> p m r u", m=M_TILES, u=2)
+            for mp in range(M_TILES // 2):
+                xt = psum.tile([P, 2, 2, P], F32, name="xt", tag="tr")
+                for mi in range(2):
                     for u in range(2):
-                        nc.tensor.transpose(xt[:, gi, u, :], words[:, 256 * g + u:256 * (g + 1):2], ident[:])
-                src = xt[:].rearrange("p g u r -> p g r u")
-                dst = gw[:, 2 * gp:2 * gp + 2, :, :]
-                if gp == 0:
+                        nc.tensor.transpose(xt[:, mi, u, :], words[:, 2 * mp + mi, u::2], ident[:])
+                src = xt[:].rearrange("p m u r -> p m r u")
+                dst = gw[:, 2 * mp:2 * mp + 2, :, :]
+                if mp == 0:
                     nc.vector.tensor_copy(out=dst, in_=src)
                 else:
                     nc.scalar.copy(out=dst, in_=src)
-            xc = xpool.tile([P, PASSES * P], U32, name="x_codes%d" % m, align_bytes=64)
-            xsc = xpool.tile([P, PASSES * P], U8, name="x_scales%d" % m, align_bytes=64)
+            xc = xpool.tile([P, TOK], U32, name="x_codes%d" % g, align_bytes=64)
+            xsc = xpool.tile([P, TOK], U8, name="x_scales%d" % g, align_bytes=64)
             nc.vector.quantize_mx(out=xc[:].bitcast(FP8X4), scales=xsc[:], in_=x_grouped[:])
             x_codes.append(xc)
             x_scales.append(xsc)
@@ -175,80 +201,90 @@ def tile_attn_pa_kernel(tc, x, W_qk_bytes, W_qk_scale, out_0, out_1):
             w_codes[s] = wc
             w_scales[s] = ws
 
-        def multiply(s):
-            c, g = divmod(s, PASSES)
-            for m in range(M_TILES):
-                if g == 0:
-                    bank = psum.tile([P, N_TILE], F32, name="acc", tag="bank")
-                    acc[(c, m)] = bank
-                cols = slice(g * P, (g + 1) * P)
+        def multiply(hd):
+            c, j = divmod(hd, HEADS_PER_CHUNK)
+            bank = psum.tile([P, TOK], F32, name="acc", tag="mx")
+            cols = slice(j * DH, (j + 1) * DH)
+            for g in range(PASSES):
+                s = c * PASSES + g
                 nc.tensor.matmul_mx(
-                    out=acc[(c, m)][:],
-                    lhsT=x_codes[m][:, cols].bitcast(FP8X4), lhsT_scale=x_scales[m][:, cols],
-                    rhs=w_codes[s][:].bitcast(FP8X4), rhs_scale=w_scales[s][:],
+                    out=bank[:],
+                    lhsT=w_codes[s][:, cols].bitcast(FP8X4), lhsT_scale=w_scales[s][:, cols],
+                    rhs=x_codes[g][:].bitcast(FP8X4), rhs_scale=x_scales[g][:],
                     start=(g == 0), stop=(g == PASSES - 1),
                 )
+            acc[hd] = bank
 
         rot = {}
+        turned = {}
+        norm = {}
 
-        def epi_rotate(e):
-            c, m = divmod(e, M_TILES)
-            a = m % 2
-            bank = acc[(c, m)]
-            ta = epi.tile([P, HEADS_PER_CHUNK, 2, HALF], F32, name="ta", bufs=6)
-            tb = epi.tile([P, HEADS_PER_CHUNK, 2, HALF], F32, name="tb", bufs=3)
-            bv = bank[:].rearrange("p (h w i) -> p h w i", w=2, i=HALF)
-            shape = [P, HEADS_PER_CHUNK, 2, HALF]
-            nc.vector.tensor_tensor(out=ta[:], in0=bv,
-                                    in1=trig[:, a, 2:3, :].unsqueeze(1).to_broadcast(shape), op=ALU.mult)
-            nc.vector.tensor_tensor(out=tb[:], in0=bv,
-                                    in1=trig[:, a, 0:2, :].unsqueeze(1).to_broadcast(shape), op=ALU.mult)
-            rot[e] = (ta, tb)
+        def rotate(hd):
+            bv = acc[hd][:].rearrange("p (b t) -> p b t", b=B)
+            ta = epi.tile([P, TOK], F32, name="ta")
+            tb = epi.tile([P, TOK], F32, name="tb")
+            shape = [P, B, T]
+            nc.vector.tensor_tensor(out=ta[:].rearrange("p (b t) -> p b t", b=B), in0=bv,
+                                    in1=tab[:, 1:2, :].to_broadcast(shape), op=ALU.mult)
+            nc.vector.tensor_tensor(out=tb[:].rearrange("p (b t) -> p b t", b=B), in0=bv,
+                                    in1=tab[:, 0:1, :].to_broadcast(shape), op=ALU.mult)
+            rot[hd] = (ta, tb)
 
-        def epi_add(e):
-            ta, tb = rot[e]
-            nc.vector.tensor_tensor(out=ta[:], in0=ta[:], in1=tb[:, :, ::-1, :], op=ALU.add)
+        def turn(hd):
+            ta, tb = rot[hd]
+            back = psum.tile([P, M_TILES, P], F32, name="back", tag="tr")
+            for m in range(M_TILES):
+                cols = slice(m * P, (m + 1) * P)
+                nc.tensor.matmul(out=back[:, m, :], lhsT=ta[:, cols], rhs=ident[:], is_transpose=True,
+                                 start=True, stop=False)
+                nc.tensor.matmul(out=back[:, m, :], lhsT=tb[:, cols], rhs=swp[:], is_transpose=True,
+                                 start=False, stop=True)
+            turned[hd] = back
 
-        def epi_scale_store(e):
-            c, m = divmod(e, M_TILES)
-            ta, tb = rot[e]
-            ss = small.tile([P, HEADS_PER_CHUNK], F32, name="ss")
-            for h in range(HEADS_PER_CHUNK):
+        def epi_norm(hd):
+            back = turned[hd]
+            ss = small.tile([P, M_TILES], F32, name="ss")
+            for m in range(M_TILES):
                 junk = small.tile([P, DH], F32, name="junk", bufs=2)
-                nc.scalar.activation(out=junk[:].rearrange("p (w i) -> p w i", w=2), in_=ta[:, h, :, :],
-                                     func=ACT.Square, accum_out=ss[:, h:h + 1])
-            r = small.tile([P, HEADS_PER_CHUNK], F32, name="r")
+                nc.scalar.activation(out=junk[:], in_=back[:, m, :], func=ACT.Square, accum_out=ss[:, m:m + 1])
+            r = small.tile([P, M_TILES], F32, name="r")
             nc.scalar.activation(out=r[:], in_=ss[:], func=ACT.Abs_reciprocal_sqrt, scale=1.0 / DH,
                                  bias=eps_col[:, 0:1])
-            for h in range(HEADS_PER_CHUNK):
-                nc.scalar.activation(out=ta[:, h, :, :], in_=ta[:, h, :, :], func=ACT.Copy, scale=r[:, h:h + 1])
-            dst = outs[c // (CHUNKS // 2)]
-            h0 = (c % (CHUNKS // 2)) * HEADS_PER_CHUNK
-            b, a = divmod(m, 2)
-            nc.sync.dma_start(
-                out=dst[b, h0:h0 + HEADS_PER_CHUNK, a * P:(a + 1) * P, :].rearrange("h t d -> t h d"),
-                in_=ta[:].rearrange("p h w i -> p h (w i)"))
+            norm[hd] = r
+
+        def epi_scale_store(hd):
+            back = turned[hd]
+            r = norm[hd]
+            res = epi.tile([P, M_TILES, DH], F32, name="res", bufs=4)
+            for m in range(M_TILES):
+                if vector_scales(hd):
+                    nc.vector.tensor_scalar(out=res[:, m, :], in0=back[:, m, :], scalar1=r[:, m:m + 1],
+                                            scalar2=None, op0=ALU.mult)
+                else:
+                    nc.scalar.activation(out=res[:, m, :], in_=back[:, m, :], func=ACT.Copy, scale=r[:, m:m + 1])
+            dst = outs[hd // H]
+            for b in range(B):
+                nc.sync.dma_start(out=dst[b, hd % H, :, :].rearrange("(a p) d -> p a d", p=P),
+                                  in_=res[:, 2 * b:2 * b + 2, :])
 
         widen(0)
         widen(1)
-        for i in range(STEPS + EPI_LAG + 1):
-            e = i - EPI_LAG
-            if 0 <= e - 1 < STEPS:
-                epi_scale_store(e - 1)
+        for i in range(STEPS + LAG_NORM):
+            if 0 <= i - LAG_NORM < HEADS:
+                epi_norm(i - LAG_NORM)
             if i + 2 < STEPS:
                 widen(i + 2)
             if i < STEPS:
                 interleave(i)
-            if i < M_TILES:
+            if i < PASSES:
                 prep_x(i)
-            if 0 <= e < STEPS:
-                epi_rotate(e)
+            if 0 <= i - LAG_MX < HEADS:
+                multiply(i - LAG_MX)
+            if 0 <= i - LAG_ROT < HEADS:
+                rotate(i - LAG_ROT)
             if i < STEPS:
                 quantize(i)
-            if i == M_TILES - 1:
-                for s in range(M_TILES):
-                    multiply(s)
-            elif M_TILES <= i < STEPS:
-                multiply(i)
-            if 0 <= e < STEPS:
-                epi_add(e)
+            if 0 <= i - LAG_ROT < HEADS:
+                turn(i - LAG_ROT)
+            if 0 <= i - LAG_NORM < HEADS:
+                epi_scale_store(i - LAG_NORM)

@@ -40,13 +40,15 @@ LAG_NORM = 6
 
 
 def vector_planes(s):
-    if s < 4:
+    if s < 6:
         return 2
+    if s < STEPS - 4 and s % 4 != 3:
+        return 1
     return 0
 
 
 def vector_scales(hd):
-    return hd % 2 == 1
+    return hd in (HEADS - 3, HEADS - 1)
 
 
 def tile_attn_pa_kernel(tc, x, W_qk_bytes, W_qk_scale, out_0, out_1):
@@ -61,7 +63,7 @@ def tile_attn_pa_kernel(tc, x, W_qk_bytes, W_qk_scale, out_0, out_1):
         wbytes = ctx.enter_context(tc.tile_pool(name="wbytes", bufs=STEPS))
         wprep = ctx.enter_context(tc.tile_pool(name="wprep", bufs=3))
         wq = ctx.enter_context(tc.tile_pool(name="wq", bufs=12))
-        epi = ctx.enter_context(tc.tile_pool(name="epi", bufs=3))
+        epi = ctx.enter_context(tc.tile_pool(name="epi", bufs=4))
         small = ctx.enter_context(tc.tile_pool(name="small", bufs=6))
         psum = ctx.enter_context(tc.psum_pool(name="psum", bufs=4))
 
@@ -136,13 +138,17 @@ def tile_attn_pa_kernel(tc, x, W_qk_bytes, W_qk_scale, out_0, out_1):
         nc.vector.memset(eps_col[:], EPS)
         warm = const.tile([P, 1], F32, name="warm")
         nc.scalar.activation(out=warm[:], in_=tau[:, 0:1], func=ACT.Abs_reciprocal_sqrt, bias=eps_col[:, 0:1])
-        tab_ps = psum.tile([P, 2, 2, P], F32, name="tab_ps", tag="tr")
-        for k in range(2):
-            for a in range(2):
-                nc.tensor.transpose(tab_ps[:, k, a, :],
-                                    trig[:, a, 2 * k:2 * k + 2, :].rearrange("p w i -> p (w i)"), ident[:])
-        tab = const.tile([P, 2, T], F32, name="tab")
-        nc.vector.tensor_copy(out=tab[:].rearrange("p k (a t) -> p k a t", a=2), in_=tab_ps[:])
+        tables = []
+
+        def turn_tables():
+            tab_ps = psum.tile([P, 2, 2, P], F32, name="tab_ps", tag="tr")
+            for k in range(2):
+                for a in range(2):
+                    nc.tensor.transpose(tab_ps[:, k, a, :],
+                                        trig[:, a, 2 * k:2 * k + 2, :].rearrange("p w i -> p (w i)"), ident[:])
+            tab = const.tile([P, 2, T], F32, name="tab")
+            nc.vector.tensor_copy(out=tab[:].rearrange("p k (a t) -> p k a t", a=2), in_=tab_ps[:])
+            tables.append(tab)
 
         x_codes = []
         x_scales = []
@@ -176,7 +182,7 @@ def tile_attn_pa_kernel(tc, x, W_qk_bytes, W_qk_scale, out_0, out_1):
 
         def widen(s):
             g = s % PASSES
-            pl = wprep.tile([P, PACK, N_TILE], BF16, name="pl", bufs=4)
+            pl = wprep.tile([P, PACK, N_TILE], BF16, name="pl", bufs=6)
             nv = vector_planes(s)
             for t in range(PACK):
                 col = sc[:, g * PACK + t:g * PACK + t + 1]
@@ -188,7 +194,7 @@ def tile_attn_pa_kernel(tc, x, W_qk_bytes, W_qk_scale, out_0, out_1):
             planes[s] = pl
 
         def interleave(s):
-            il = wprep.tile([P, N_TILE, PACK], BF16, name="il", align_bytes=64)
+            il = wprep.tile([P, N_TILE, PACK], BF16, name="il", align_bytes=64, bufs=4)
             nc.vector.tensor_copy(out=il[:].rearrange("p (c i) t -> p c t i", i=4),
                                   in_=planes[s][:].rearrange("p t (c i) -> p c t i", i=4))
             grouped[s] = il
@@ -225,9 +231,9 @@ def tile_attn_pa_kernel(tc, x, W_qk_bytes, W_qk_scale, out_0, out_1):
             tb = epi.tile([P, TOK], F32, name="tb")
             shape = [P, B, T]
             nc.vector.tensor_tensor(out=ta[:].rearrange("p (b t) -> p b t", b=B), in0=bv,
-                                    in1=tab[:, 1:2, :].to_broadcast(shape), op=ALU.mult)
+                                    in1=tables[0][:, 1:2, :].to_broadcast(shape), op=ALU.mult)
             nc.vector.tensor_tensor(out=tb[:].rearrange("p (b t) -> p b t", b=B), in0=bv,
-                                    in1=tab[:, 0:1, :].to_broadcast(shape), op=ALU.mult)
+                                    in1=tables[0][:, 0:1, :].to_broadcast(shape), op=ALU.mult)
             rot[hd] = (ta, tb)
 
         def turn(hd):
@@ -269,15 +275,18 @@ def tile_attn_pa_kernel(tc, x, W_qk_bytes, W_qk_scale, out_0, out_1):
 
         widen(0)
         widen(1)
+        widen(2)
         for i in range(STEPS + LAG_NORM):
             if 0 <= i - LAG_NORM < HEADS:
                 epi_norm(i - LAG_NORM)
-            if i + 2 < STEPS:
-                widen(i + 2)
+            if i + 3 < STEPS:
+                widen(i + 3)
             if i < STEPS:
                 interleave(i)
             if i < PASSES:
                 prep_x(i)
+            if i == PASSES - 1:
+                turn_tables()
             if 0 <= i - LAG_MX < HEADS:
                 multiply(i - LAG_MX)
             if 0 <= i - LAG_ROT < HEADS:

@@ -40,8 +40,10 @@ LAG_NORM = 6
 
 
 def vector_planes(s):
-    if s < 6:
+    if s < 3:
         return 2
+    if s < 7:
+        return 0
     if s < STEPS - 4 and s % 4 != 3:
         return 1
     return 0
@@ -164,10 +166,7 @@ def tile_attn_pa_kernel(tc, x, W_qk_bytes, W_qk_scale, out_0, out_1):
                         nc.tensor.transpose(xt[:, mi, u, :], words[:, 2 * mp + mi, u::2], ident[:])
                 src = xt[:].rearrange("p m u r -> p m r u")
                 dst = gw[:, 2 * mp:2 * mp + 2, :, :]
-                if mp == 0:
-                    nc.vector.tensor_copy(out=dst, in_=src)
-                else:
-                    nc.scalar.copy(out=dst, in_=src)
+                nc.scalar.copy(out=dst, in_=src)
             xc = xpool.tile([P, TOK], U32, name="x_codes%d" % g, align_bytes=64)
             xsc = xpool.tile([P, TOK], U8, name="x_scales%d" % g, align_bytes=64)
             nc.vector.quantize_mx(out=xc[:].bitcast(FP8X4), scales=xsc[:], in_=x_grouped[:])

@@ -42,11 +42,7 @@ LAG_NORM = 6
 def vector_planes(s):
     if s < 3:
         return 2
-    if s < 7:
-        return 0
-    if s < STEPS - 4 and s % 4 != 3:
-        return 1
-    return 0
+    return 1
 
 
 def vector_scales(hd):
@@ -97,6 +93,10 @@ def tile_attn_pa_kernel(tc, x, W_qk_bytes, W_qk_scale, out_0, out_1):
         for s in range(PASSES, STEPS):
             load_w(s)
 
+        zero = const.tile([P, 1], F32, name="zero")
+        nc.vector.memset(zero[:], 0.0)
+        warm = const.tile([P, 1], F32, name="warm")
+        nc.scalar.activation(out=warm[:], in_=zero[:], func=ACT.Sin)
         ident = const.tile([P, P], F32, name="ident")
         make_identity(nc, ident[:])
         swp = const.tile([P, P], F32, name="swp")
@@ -138,8 +138,6 @@ def tile_attn_pa_kernel(tc, x, W_qk_bytes, W_qk_scale, out_0, out_1):
         nc.scalar.activation(out=trig[:, :, 3, :], in_=frac[:, :, 1, :], func=ACT.Sin, scale=2.0 * math.pi)
         eps_col = const.tile([P, 1], F32, name="eps_col")
         nc.vector.memset(eps_col[:], EPS)
-        warm = const.tile([P, 1], F32, name="warm")
-        nc.scalar.activation(out=warm[:], in_=tau[:, 0:1], func=ACT.Abs_reciprocal_sqrt, bias=eps_col[:, 0:1])
         tables = []
 
         def turn_tables():
@@ -225,24 +223,21 @@ def tile_attn_pa_kernel(tc, x, W_qk_bytes, W_qk_scale, out_0, out_1):
         norm = {}
 
         def rotate(hd):
-            bv = acc[hd][:].rearrange("p (b t) -> p b t", b=B)
-            ta = epi.tile([P, TOK], F32, name="ta")
-            tb = epi.tile([P, TOK], F32, name="tb")
-            shape = [P, B, T]
-            nc.vector.tensor_tensor(out=ta[:].rearrange("p (b t) -> p b t", b=B), in0=bv,
-                                    in1=tables[0][:, 1:2, :].to_broadcast(shape), op=ALU.mult)
-            nc.vector.tensor_tensor(out=tb[:].rearrange("p (b t) -> p b t", b=B), in0=bv,
-                                    in1=tables[0][:, 0:1, :].to_broadcast(shape), op=ALU.mult)
-            rot[hd] = (ta, tb)
+            shape = [P, 2, B, T]
+            prod = epi.tile([P, 2, TOK], F32, name="prod")
+            nc.vector.tensor_tensor(out=prod[:].rearrange("p k (b t) -> p k b t", b=B),
+                                    in0=acc[hd][:].rearrange("p (b t) -> p b t", b=B).unsqueeze(1).to_broadcast(shape),
+                                    in1=tables[0][:].unsqueeze(2).to_broadcast(shape), op=ALU.mult)
+            rot[hd] = prod
 
         def turn(hd):
-            ta, tb = rot[hd]
+            prod = rot[hd]
             back = psum.tile([P, M_TILES, P], F32, name="back", tag="tr")
             for m in range(M_TILES):
                 cols = slice(m * P, (m + 1) * P)
-                nc.tensor.matmul(out=back[:, m, :], lhsT=ta[:, cols], rhs=ident[:], is_transpose=True,
+                nc.tensor.matmul(out=back[:, m, :], lhsT=prod[:, 1, cols], rhs=ident[:], is_transpose=True,
                                  start=True, stop=False)
-                nc.tensor.matmul(out=back[:, m, :], lhsT=tb[:, cols], rhs=swp[:], is_transpose=True,
+                nc.tensor.matmul(out=back[:, m, :], lhsT=prod[:, 0, cols], rhs=swp[:], is_transpose=True,
                                  start=False, stop=True)
             turned[hd] = back
 

@@ -46,7 +46,7 @@ def vector_planes(s):
 
 
 def vector_scales(hd):
-    return hd in (HEADS - 3, HEADS - 1)
+    return hd >= HEADS - 4
 
 
 def tile_attn_pa_kernel(tc, x, W_qk_bytes, W_qk_scale, out_0, out_1):
@@ -84,13 +84,12 @@ def tile_attn_pa_kernel(tc, x, W_qk_bytes, W_qk_scale, out_0, out_1):
             nc.sync.dma_start(out=x_rows[:], in_=xv[:, :, g * K_PASS:(g + 1) * K_PASS])
             xs.append(x_rows)
 
-        load_w(0)
-        load_w(1)
+        for s in range(3):
+            load_w(s)
         for g in range(PASSES):
             load_x(g)
-            if g + 2 < PASSES:
-                load_w(g + 2)
-        for s in range(PASSES, STEPS):
+            load_w(g + 3)
+        for s in range(PASSES + 3, STEPS):
             load_w(s)
 
         zero = const.tile([P, 1], F32, name="zero")
@@ -221,73 +220,94 @@ def tile_attn_pa_kernel(tc, x, W_qk_bytes, W_qk_scale, out_0, out_1):
         rot = {}
         turned = {}
         norm = {}
+        BOTH = (0, 1)
 
-        def rotate(hd):
-            shape = [P, 2, B, T]
-            prod = epi.tile([P, 2, TOK], F32, name="prod")
-            nc.vector.tensor_tensor(out=prod[:].rearrange("p k (b t) -> p k b t", b=B),
-                                    in0=acc[hd][:].rearrange("p (b t) -> p b t", b=B).unsqueeze(1).to_broadcast(shape),
+        def rotate(hd, bs=BOTH):
+            toks = slice(bs[0] * T, (bs[-1] + 1) * T)
+            shape = [P, 2, len(bs), T]
+            prod = epi.tile([P, 2, len(bs) * T], F32, name="prod")
+            nc.vector.tensor_tensor(out=prod[:].rearrange("p k (b t) -> p k b t", t=T),
+                                    in0=acc[hd][:, toks].rearrange("p (b t) -> p b t", t=T).unsqueeze(1).to_broadcast(shape),
                                     in1=tables[0][:].unsqueeze(2).to_broadcast(shape), op=ALU.mult)
-            rot[hd] = prod
+            rot[(hd, bs)] = prod
 
-        def turn(hd):
-            prod = rot[hd]
-            back = psum.tile([P, M_TILES, P], F32, name="back", tag="tr")
-            for m in range(M_TILES):
+        def turn(hd, bs=BOTH, tag="tr"):
+            prod = rot[(hd, bs)]
+            back = psum.tile([P, 2 * len(bs), P], F32, name="back", tag=tag)
+            for m in range(2 * len(bs)):
                 cols = slice(m * P, (m + 1) * P)
                 nc.tensor.matmul(out=back[:, m, :], lhsT=prod[:, 1, cols], rhs=ident[:], is_transpose=True,
                                  start=True, stop=False)
                 nc.tensor.matmul(out=back[:, m, :], lhsT=prod[:, 0, cols], rhs=swp[:], is_transpose=True,
                                  start=False, stop=True)
-            turned[hd] = back
+            turned[(hd, bs)] = back
 
-        def epi_norm(hd):
-            back = turned[hd]
-            ss = small.tile([P, M_TILES], F32, name="ss")
-            for m in range(M_TILES):
+        def epi_norm(hd, bs=BOTH):
+            back = turned[(hd, bs)]
+            ss = small.tile([P, 2 * len(bs)], F32, name="ss")
+            for m in range(2 * len(bs)):
                 junk = small.tile([P, DH], F32, name="junk", bufs=2)
                 nc.scalar.activation(out=junk[:], in_=back[:, m, :], func=ACT.Square, accum_out=ss[:, m:m + 1])
-            r = small.tile([P, M_TILES], F32, name="r")
+            r = small.tile([P, 2 * len(bs)], F32, name="r")
             nc.scalar.activation(out=r[:], in_=ss[:], func=ACT.Abs_reciprocal_sqrt, scale=1.0 / DH,
                                  bias=eps_col[:, 0:1])
-            norm[hd] = r
+            norm[(hd, bs)] = r
 
-        def epi_scale_store(hd):
-            back = turned[hd]
-            r = norm[hd]
-            res = epi.tile([P, M_TILES, DH], F32, name="res", bufs=4)
-            for m in range(M_TILES):
+        def epi_scale_store(hd, bs=BOTH):
+            back = turned[(hd, bs)]
+            r = norm[(hd, bs)]
+            res = epi.tile([P, 2 * len(bs), DH], F32, name="res", bufs=4)
+            for m in range(2 * len(bs)):
                 if vector_scales(hd):
                     nc.vector.tensor_scalar(out=res[:, m, :], in0=back[:, m, :], scalar1=r[:, m:m + 1],
                                             scalar2=None, op0=ALU.mult)
                 else:
                     nc.scalar.activation(out=res[:, m, :], in_=back[:, m, :], func=ACT.Copy, scale=r[:, m:m + 1])
             dst = outs[hd // H]
-            for b in range(B):
-                nc.sync.dma_start(out=dst[b, hd % H, :, :].rearrange("(a p) d -> p a d", p=P),
-                                  in_=res[:, 2 * b:2 * b + 2, :])
+            for k in range(len(bs)):
+                nc.sync.dma_start(out=dst[bs[k], hd % H, :, :].rearrange("(a p) d -> p a d", p=P),
+                                  in_=res[:, 2 * k:2 * k + 2, :])
 
         widen(0)
         widen(1)
         widen(2)
-        for i in range(STEPS + LAG_NORM):
-            if 0 <= i - LAG_NORM < HEADS:
+        for i in range(STEPS):
+            if 0 <= i - LAG_NORM:
                 epi_norm(i - LAG_NORM)
             if i + 3 < STEPS:
                 widen(i + 3)
-            if i < STEPS:
-                interleave(i)
+            interleave(i)
             if i < PASSES:
                 prep_x(i)
             if i == PASSES - 1:
                 turn_tables()
-            if 0 <= i - LAG_MX < HEADS:
+            if 0 <= i - LAG_MX:
                 multiply(i - LAG_MX)
-            if 0 <= i - LAG_ROT < HEADS:
+            if 0 <= i - LAG_ROT:
                 rotate(i - LAG_ROT)
-            if i < STEPS:
-                quantize(i)
-            if 0 <= i - LAG_ROT < HEADS:
+            quantize(i)
+            if 0 <= i - LAG_ROT:
                 turn(i - LAG_ROT)
-            if 0 <= i - LAG_NORM < HEADS:
+            if 0 <= i - LAG_NORM:
                 epi_scale_store(i - LAG_NORM)
+        for hd in range(STEPS - LAG_MX, HEADS - 1):
+            multiply(hd)
+        rotate(STEPS - LAG_ROT)
+        turn(STEPS - LAG_ROT)
+        multiply(HEADS - 1)
+        for hd in range(STEPS - LAG_ROT + 1, HEADS - 1):
+            rotate(hd)
+            turn(hd)
+            if hd - 2 < STEPS - LAG_MX:
+                epi_norm(hd - 2)
+                epi_scale_store(hd - 2)
+        rotate(HEADS - 1, (0,))
+        turn(HEADS - 1, (0,))
+        rotate(HEADS - 1, (1,))
+        turn(HEADS - 1, (1,), "mx")
+        for hd in range(STEPS - LAG_MX, HEADS - 1):
+            epi_norm(hd)
+            epi_scale_store(hd)
+        for b in range(B):
+            epi_norm(HEADS - 1, (b,))
+            epi_scale_store(HEADS - 1, (b,))

@@ -42,6 +42,8 @@ LAG_NORM = 6
 def vector_planes(s):
     if s < 3:
         return 2
+    if s % 8 == 7:
+        return 0
     return 1
 
 
@@ -60,7 +62,7 @@ def tile_attn_pa_kernel(tc, x, W_qk_bytes, W_qk_scale, out_0, out_1):
         xpool = ctx.enter_context(tc.tile_pool(name="xpool", bufs=1))
         wbytes = ctx.enter_context(tc.tile_pool(name="wbytes", bufs=STEPS))
         wprep = ctx.enter_context(tc.tile_pool(name="wprep", bufs=3))
-        wq = ctx.enter_context(tc.tile_pool(name="wq", bufs=12))
+        wq = ctx.enter_context(tc.tile_pool(name="wq", bufs=6))
         epi = ctx.enter_context(tc.tile_pool(name="epi", bufs=4))
         small = ctx.enter_context(tc.tile_pool(name="small", bufs=6))
         psum = ctx.enter_context(tc.psum_pool(name="psum", bufs=4))
@@ -190,28 +192,30 @@ def tile_attn_pa_kernel(tc, x, W_qk_bytes, W_qk_scale, out_0, out_1):
             planes[s] = pl
 
         def interleave(s):
-            il = wprep.tile([P, N_TILE, PACK], BF16, name="il", align_bytes=64, bufs=4)
-            nc.vector.tensor_copy(out=il[:].rearrange("p (c i) t -> p c t i", i=4),
+            if s % 2 == 0:
+                pair = wprep.tile([P, 2, N_TILE, PACK], BF16, name="il", align_bytes=64, bufs=3)
+                grouped[s // 2] = pair
+            il = grouped[s // 2][:, s % 2, :, :]
+            nc.vector.tensor_copy(out=il.rearrange("p (c i) t -> p c t i", i=4),
                                   in_=planes[s][:].rearrange("p t (c i) -> p c t i", i=4))
-            grouped[s] = il
 
-        def quantize(s):
-            wc = wq.tile([P, N_TILE], U32, name="wc", align_bytes=64)
-            ws = wq.tile([P, N_TILE], U8, name="ws", align_bytes=64)
+        def quantize(j):
+            wc = wq.tile([P, 2 * N_TILE], U32, name="wc", align_bytes=64)
+            ws = wq.tile([P, 2 * N_TILE], U8, name="ws", align_bytes=64)
             nc.vector.quantize_mx(out=wc[:].bitcast(FP8X4), scales=ws[:],
-                                  in_=grouped[s][:].rearrange("p n t -> p (n t)"))
-            w_codes[s] = wc
-            w_scales[s] = ws
+                                  in_=grouped[j][:].rearrange("p s n t -> p (s n t)"))
+            w_codes[j] = wc
+            w_scales[j] = ws
 
         def multiply(hd):
             c, j = divmod(hd, HEADS_PER_CHUNK)
             bank = psum.tile([P, TOK], F32, name="acc", tag="mx")
-            cols = slice(j * DH, (j + 1) * DH)
             for g in range(PASSES):
                 s = c * PASSES + g
+                cols = slice((s % 2) * N_TILE + j * DH, (s % 2) * N_TILE + (j + 1) * DH)
                 nc.tensor.matmul_mx(
                     out=bank[:],
-                    lhsT=w_codes[s][:, cols].bitcast(FP8X4), lhsT_scale=w_scales[s][:, cols],
+                    lhsT=w_codes[s // 2][:, cols].bitcast(FP8X4), lhsT_scale=w_scales[s // 2][:, cols],
                     rhs=x_codes[g][:].bitcast(FP8X4), rhs_scale=x_scales[g][:],
                     start=(g == 0), stop=(g == PASSES - 1),
                 )
@@ -285,7 +289,8 @@ def tile_attn_pa_kernel(tc, x, W_qk_bytes, W_qk_scale, out_0, out_1):
                 multiply(i - LAG_MX)
             if 0 <= i - LAG_ROT:
                 rotate(i - LAG_ROT)
-            quantize(i)
+            if i % 2 == 1:
+                quantize(i // 2)
             if 0 <= i - LAG_ROT:
                 turn(i - LAG_ROT)
             if 0 <= i - LAG_NORM:

@@ -37,12 +37,15 @@ HEADS = 2 * H
 LAG_MX = 4
 LAG_ROT = 5
 LAG_NORM = 6
+PIN_FROM = 6
+G_COLS = 96
+G_FROM = 10
 
 
 def vector_planes(s):
     if s < 3:
         return 2
-    if s % 8 == 7:
+    if s < G_FROM and s % 8 == 7:
         return 0
     return 1
 
@@ -178,26 +181,37 @@ def tile_attn_pa_kernel(tc, x, W_qk_bytes, W_qk_scale, out_0, out_1):
         w_scales = {}
         acc = {}
 
-        def widen(s):
+        def widen_scalar(s):
             g = s % PASSES
-            pl = wprep.tile([P, PACK, N_TILE], BF16, name="pl", bufs=6)
-            nv = vector_planes(s)
-            for t in range(PACK):
-                col = sc[:, g * PACK + t:g * PACK + t + 1]
-                src = wb[s][:, t, :].bitcast(FP8)
-                if t < nv:
-                    nc.vector.tensor_scalar(out=pl[:, t, :], in0=src, scalar1=col, scalar2=None, op0=ALU.mult)
-                else:
-                    nc.scalar.activation(out=pl[:, t, :], in_=src, func=ACT.Copy, scale=col)
+            pl = wprep.tile([P, PACK, N_TILE], BF16, name="pl", bufs=7)
+            for t in range(vector_planes(s), PACK):
+                nc.scalar.activation(out=pl[:, t, :], in_=wb[s][:, t, :].bitcast(FP8), func=ACT.Copy,
+                                     scale=sc[:, g * PACK + t:g * PACK + t + 1])
             planes[s] = pl
 
-        def interleave(s):
-            if s % 2 == 0:
-                pair = wprep.tile([P, 2, N_TILE, PACK], BF16, name="il", align_bytes=64, bufs=3)
+        def widen_vector(s):
+            g = s % PASSES
+            for t in range(vector_planes(s)):
+                nc.vector.tensor_scalar(out=planes[s][:, t, :], in0=wb[s][:, t, :].bitcast(FP8),
+                                        scalar1=sc[:, g * PACK + t:g * PACK + t + 1], scalar2=None, op0=ALU.mult)
+
+        def pair_tile(s):
+            if s // 2 not in grouped:
+                pair = wprep.tile([P, 2, N_TILE, PACK], BF16, name="il", align_bytes=64, bufs=4)
                 grouped[s // 2] = pair
-            il = grouped[s // 2][:, s % 2, :, :]
-            nc.vector.tensor_copy(out=il.rearrange("p (c i) t -> p c t i", i=4),
-                                  in_=planes[s][:].rearrange("p t (c i) -> p c t i", i=4))
+            return grouped[s // 2][:, s % 2, :, :]
+
+        def interleave_gpsimd(s):
+            il = pair_tile(s)
+            nc.gpsimd.tensor_scalar(out=il[:, N_TILE - G_COLS:, :],
+                                    in0=planes[s][:, :, N_TILE - G_COLS:].rearrange("p t n -> p n t"),
+                                    scalar1=1.0, scalar2=0.0, op0=ALU.mult, op1=ALU.add)
+
+        def interleave(s):
+            il = pair_tile(s)
+            n = N_TILE - G_COLS if s >= G_FROM else N_TILE
+            nc.vector.tensor_copy(out=il[:, 0:n, :].rearrange("p (c i) t -> p c t i", i=4),
+                                  in_=planes[s][:, :, 0:n].rearrange("p t (c i) -> p c t i", i=4))
 
         def quantize(j):
             wc = wq.tile([P, 2 * N_TILE], U32, name="wc", align_bytes=64)
@@ -272,14 +286,15 @@ def tile_attn_pa_kernel(tc, x, W_qk_bytes, W_qk_scale, out_0, out_1):
                 nc.sync.dma_start(out=dst[bs[k], hd % H, :, :].rearrange("(a p) d -> p a d", p=P),
                                   in_=res[:, 2 * k:2 * k + 2, :])
 
-        widen(0)
-        widen(1)
-        widen(2)
-        for i in range(STEPS):
+        for s in range(3):
+            widen_scalar(s)
+            widen_vector(s)
+        widen_scalar(3)
+        def one_round(i):
             if 0 <= i - LAG_NORM:
                 epi_norm(i - LAG_NORM)
-            if i + 3 < STEPS:
-                widen(i + 3)
+            if i + 4 < STEPS:
+                widen_scalar(i + 4)
             interleave(i)
             if i < PASSES:
                 prep_x(i)
@@ -287,6 +302,10 @@ def tile_attn_pa_kernel(tc, x, W_qk_bytes, W_qk_scale, out_0, out_1):
                 turn_tables()
             if 0 <= i - LAG_MX:
                 multiply(i - LAG_MX)
+            if i + 3 < STEPS:
+                widen_vector(i + 3)
+                if i + 3 >= G_FROM:
+                    interleave_gpsimd(i + 3)
             if 0 <= i - LAG_ROT:
                 rotate(i - LAG_ROT)
             if i % 2 == 1:
@@ -295,6 +314,11 @@ def tile_attn_pa_kernel(tc, x, W_qk_bytes, W_qk_scale, out_0, out_1):
                 turn(i - LAG_ROT)
             if 0 <= i - LAG_NORM:
                 epi_scale_store(i - LAG_NORM)
+        for i in range(PIN_FROM):
+            one_round(i)
+        with tc.manual_schedule(engines={mybir.EngineType.DVE, mybir.EngineType.Pool}):
+            for i in range(PIN_FROM, STEPS):
+                one_round(i)
         for hd in range(STEPS - LAG_MX, HEADS - 1):
             multiply(hd)
         rotate(STEPS - LAG_ROT)

@@ -38,20 +38,22 @@ LAG_MX = 4
 LAG_ROT = 5
 LAG_NORM = 6
 PIN_FROM = 6
-G_COLS = 96
-G_FROM = 10
+G_COLS = 192
+G_LAP = 4
+G_FROM = 6
+LAG_SCALE = 7
 
 
 def vector_planes(s):
     if s < 3:
         return 2
-    if s < G_FROM and s % 8 == 7:
+    if s >= 10 or s == 7:
         return 0
     return 1
 
 
 def vector_scales(hd):
-    return hd >= HEADS - 4
+    return hd < HEADS - 3
 
 
 def tile_attn_pa_kernel(tc, x, W_qk_bytes, W_qk_scale, out_0, out_1):
@@ -197,14 +199,14 @@ def tile_attn_pa_kernel(tc, x, W_qk_bytes, W_qk_scale, out_0, out_1):
 
         def pair_tile(s):
             if s // 2 not in grouped:
-                pair = wprep.tile([P, 2, N_TILE, PACK], BF16, name="il", align_bytes=64, bufs=4)
+                pair = wprep.tile([P, 2, N_TILE, PACK], BF16, name="il", align_bytes=64, bufs=3)
                 grouped[s // 2] = pair
             return grouped[s // 2][:, s % 2, :, :]
 
         def interleave_gpsimd(s):
             il = pair_tile(s)
-            nc.gpsimd.tensor_scalar(out=il[:, N_TILE - G_COLS:, :],
-                                    in0=planes[s][:, :, N_TILE - G_COLS:].rearrange("p t n -> p n t"),
+            nc.gpsimd.tensor_scalar(out=il[:, N_TILE - G_COLS - G_LAP:, :],
+                                    in0=planes[s][:, :, N_TILE - G_COLS - G_LAP:].rearrange("p t n -> p n t"),
                                     scalar1=1.0, scalar2=0.0, op0=ALU.mult, op1=ALU.add)
 
         def interleave(s):
@@ -275,11 +277,11 @@ def tile_attn_pa_kernel(tc, x, W_qk_bytes, W_qk_scale, out_0, out_1):
             back = turned[(hd, bs)]
             r = norm[(hd, bs)]
             res = epi.tile([P, 2 * len(bs), DH], F32, name="res", bufs=4)
-            for m in range(2 * len(bs)):
-                if vector_scales(hd):
-                    nc.vector.tensor_scalar(out=res[:, m, :], in0=back[:, m, :], scalar1=r[:, m:m + 1],
-                                            scalar2=None, op0=ALU.mult)
-                else:
+            if vector_scales(hd):
+                nc.vector.tensor_tensor(out=res[:], in0=back[:],
+                                        in1=r[:].unsqueeze(2).to_broadcast([P, 2 * len(bs), DH]), op=ALU.mult)
+            else:
+                for m in range(2 * len(bs)):
                     nc.scalar.activation(out=res[:, m, :], in_=back[:, m, :], func=ACT.Copy, scale=r[:, m:m + 1])
             dst = outs[hd // H]
             for k in range(len(bs)):
@@ -291,52 +293,35 @@ def tile_attn_pa_kernel(tc, x, W_qk_bytes, W_qk_scale, out_0, out_1):
             widen_vector(s)
         widen_scalar(3)
         def one_round(i):
-            if 0 <= i - LAG_NORM:
+            if 0 <= i - LAG_NORM < HEADS:
                 epi_norm(i - LAG_NORM)
             if i + 4 < STEPS:
                 widen_scalar(i + 4)
-            interleave(i)
+            if i + 3 < STEPS:
+                widen_vector(i + 3)
+            if i < STEPS:
+                interleave(i)
+                if i >= G_FROM:
+                    interleave_gpsimd(i)
             if i < PASSES:
                 prep_x(i)
             if i == PASSES - 1:
                 turn_tables()
-            if 0 <= i - LAG_MX:
+            if 0 <= i - LAG_MX < HEADS:
                 multiply(i - LAG_MX)
-            if i + 3 < STEPS:
-                widen_vector(i + 3)
-                if i + 3 >= G_FROM:
-                    interleave_gpsimd(i + 3)
-            if 0 <= i - LAG_ROT:
+            if 0 <= i - LAG_ROT < HEADS:
                 rotate(i - LAG_ROT)
-            if i % 2 == 1:
+            if 0 <= i - LAG_SCALE < HEADS:
+                epi_scale_store(i - LAG_SCALE)
+            if i < STEPS and i % 2 == 1:
                 quantize(i // 2)
-            if 0 <= i - LAG_ROT:
+            if 0 <= i - LAG_ROT < HEADS:
                 turn(i - LAG_ROT)
-            if 0 <= i - LAG_NORM:
-                epi_scale_store(i - LAG_NORM)
+
         for i in range(PIN_FROM):
             one_round(i)
         with tc.manual_schedule(engines={mybir.EngineType.DVE, mybir.EngineType.Pool}):
             for i in range(PIN_FROM, STEPS):
                 one_round(i)
-        for hd in range(STEPS - LAG_MX, HEADS - 1):
-            multiply(hd)
-        rotate(STEPS - LAG_ROT)
-        turn(STEPS - LAG_ROT)
-        multiply(HEADS - 1)
-        for hd in range(STEPS - LAG_ROT + 1, HEADS - 1):
-            rotate(hd)
-            turn(hd)
-            if hd - 2 < STEPS - LAG_MX:
-                epi_norm(hd - 2)
-                epi_scale_store(hd - 2)
-        rotate(HEADS - 1, (0,))
-        turn(HEADS - 1, (0,))
-        rotate(HEADS - 1, (1,))
-        turn(HEADS - 1, (1,), "mx")
-        for hd in range(STEPS - LAG_MX, HEADS - 1):
-            epi_norm(hd)
-            epi_scale_store(hd)
-        for b in range(B):
-            epi_norm(HEADS - 1, (b,))
-            epi_scale_store(HEADS - 1, (b,))
+        for i in range(STEPS, STEPS + LAG_SCALE):
+            one_round(i)

@@ -38,7 +38,7 @@ LAG_MX = 4
 LAG_ROT = 5
 LAG_NORM = 6
 PIN_FROM = 6
-G_COLS = 192
+G_COLS = 256
 G_LAP = 4
 G_FROM = 6
 LAG_SCALE = 7
@@ -53,7 +53,7 @@ def vector_planes(s):
 
 
 def vector_scales(hd):
-    return hd < HEADS - 3
+    return hd not in (26, 28, 30)
 
 
 def tile_attn_pa_kernel(tc, x, W_qk_bytes, W_qk_scale, out_0, out_1):
@@ -67,7 +67,7 @@ def tile_attn_pa_kernel(tc, x, W_qk_bytes, W_qk_scale, out_0, out_1):
         xpool = ctx.enter_context(tc.tile_pool(name="xpool", bufs=1))
         wbytes = ctx.enter_context(tc.tile_pool(name="wbytes", bufs=STEPS))
         wprep = ctx.enter_context(tc.tile_pool(name="wprep", bufs=3))
-        wq = ctx.enter_context(tc.tile_pool(name="wq", bufs=6))
+        wq = ctx.enter_context(tc.tile_pool(name="wq", bufs=12))
         epi = ctx.enter_context(tc.tile_pool(name="epi", bufs=4))
         small = ctx.enter_context(tc.tile_pool(name="small", bufs=6))
         psum = ctx.enter_context(tc.psum_pool(name="psum", bufs=4))
@@ -198,10 +198,10 @@ def tile_attn_pa_kernel(tc, x, W_qk_bytes, W_qk_scale, out_0, out_1):
                                         scalar1=sc[:, g * PACK + t:g * PACK + t + 1], scalar2=None, op0=ALU.mult)
 
         def pair_tile(s):
-            if s // 2 not in grouped:
-                pair = wprep.tile([P, 2, N_TILE, PACK], BF16, name="il", align_bytes=64, bufs=3)
-                grouped[s // 2] = pair
-            return grouped[s // 2][:, s % 2, :, :]
+            if s not in grouped:
+                il = wprep.tile([P, N_TILE, PACK], BF16, name="il", align_bytes=64, bufs=4)
+                grouped[s] = il
+            return grouped[s]
 
         def interleave_gpsimd(s):
             il = pair_tile(s)
@@ -216,10 +216,10 @@ def tile_attn_pa_kernel(tc, x, W_qk_bytes, W_qk_scale, out_0, out_1):
                                   in_=planes[s][:, :, 0:n].rearrange("p t (c i) -> p c t i", i=4))
 
         def quantize(j):
-            wc = wq.tile([P, 2 * N_TILE], U32, name="wc", align_bytes=64)
-            ws = wq.tile([P, 2 * N_TILE], U8, name="ws", align_bytes=64)
+            wc = wq.tile([P, N_TILE], U32, name="wc", align_bytes=64)
+            ws = wq.tile([P, N_TILE], U8, name="ws", align_bytes=64)
             nc.vector.quantize_mx(out=wc[:].bitcast(FP8X4), scales=ws[:],
-                                  in_=grouped[j][:].rearrange("p s n t -> p (s n t)"))
+                                  in_=grouped[j][:].rearrange("p n t -> p (n t)"))
             w_codes[j] = wc
             w_scales[j] = ws
 
@@ -228,10 +228,10 @@ def tile_attn_pa_kernel(tc, x, W_qk_bytes, W_qk_scale, out_0, out_1):
             bank = psum.tile([P, TOK], F32, name="acc", tag="mx")
             for g in range(PASSES):
                 s = c * PASSES + g
-                cols = slice((s % 2) * N_TILE + j * DH, (s % 2) * N_TILE + (j + 1) * DH)
+                cols = slice(j * DH, (j + 1) * DH)
                 nc.tensor.matmul_mx(
                     out=bank[:],
-                    lhsT=w_codes[s // 2][:, cols].bitcast(FP8X4), lhsT_scale=w_scales[s // 2][:, cols],
+                    lhsT=w_codes[s][:, cols].bitcast(FP8X4), lhsT_scale=w_scales[s][:, cols],
                     rhs=x_codes[g][:].bitcast(FP8X4), rhs_scale=x_scales[g][:],
                     start=(g == 0), stop=(g == PASSES - 1),
                 )
@@ -307,14 +307,14 @@ def tile_attn_pa_kernel(tc, x, W_qk_bytes, W_qk_scale, out_0, out_1):
                 prep_x(i)
             if i == PASSES - 1:
                 turn_tables()
+            if i >= 1:
+                quantize(i - 1)
             if 0 <= i - LAG_MX < HEADS:
                 multiply(i - LAG_MX)
             if 0 <= i - LAG_ROT < HEADS:
                 rotate(i - LAG_ROT)
             if 0 <= i - LAG_SCALE < HEADS:
                 epi_scale_store(i - LAG_SCALE)
-            if i < STEPS and i % 2 == 1:
-                quantize(i // 2)
             if 0 <= i - LAG_ROT < HEADS:
                 turn(i - LAG_ROT)
 
@@ -323,5 +323,16 @@ def tile_attn_pa_kernel(tc, x, W_qk_bytes, W_qk_scale, out_0, out_1):
         with tc.manual_schedule(engines={mybir.EngineType.DVE, mybir.EngineType.Pool}):
             for i in range(PIN_FROM, STEPS):
                 one_round(i)
-        for i in range(STEPS, STEPS + LAG_SCALE):
-            one_round(i)
+        quantize(STEPS - 1)
+        for hd in range(STEPS - LAG_MX, HEADS - 1):
+            multiply(hd)
+        rotate(STEPS - LAG_ROT)
+        turn(STEPS - LAG_ROT)
+        multiply(HEADS - 1)
+        for hd in range(STEPS - LAG_ROT + 1, HEADS + 3):
+            if hd - 2 < HEADS:
+                epi_norm(hd - 2)
+            if hd < HEADS:
+                rotate(hd)
+                turn(hd)
+            epi_scale_store(hd - 3)

@@ -37,10 +37,9 @@ HEADS = 2 * H
 LAG_MX = 4
 LAG_ROT = 5
 LAG_NORM = 6
-PIN_FROM = 6
-G_COLS = 256
+PIN_FROM = 5
 G_LAP = 4
-G_FROM = 6
+G_FROM = 5
 LAG_SCALE = 7
 
 
@@ -53,7 +52,15 @@ def vector_planes(s):
 
 
 def vector_scales(hd):
-    return hd not in (26, 28, 30)
+    return hd < 21 or hd >= 28
+
+
+def gpsimd_columns(s):
+    if s < G_FROM:
+        return 0
+    if s >= LAG_SCALE and vector_scales(s - LAG_SCALE):
+        return 256
+    return 192
 
 
 def tile_attn_pa_kernel(tc, x, W_qk_bytes, W_qk_scale, out_0, out_1):
@@ -155,6 +162,9 @@ def tile_attn_pa_kernel(tc, x, W_qk_bytes, W_qk_scale, out_0, out_1):
             tab = const.tile([P, 2, T], F32, name="tab")
             nc.vector.tensor_copy(out=tab[:].rearrange("p k (a t) -> p k a t", a=2), in_=tab_ps[:])
             tables.append(tab)
+            warm_root = const.tile([P, 1], F32, name="warm_root")
+            nc.scalar.activation(out=warm_root[:], in_=trig[:, 1, 3, 0:1], func=ACT.Abs_reciprocal_sqrt, scale=0.0,
+                                 bias=eps_col[:, 0:1])
 
         x_codes = []
         x_scales = []
@@ -205,13 +215,14 @@ def tile_attn_pa_kernel(tc, x, W_qk_bytes, W_qk_scale, out_0, out_1):
 
         def interleave_gpsimd(s):
             il = pair_tile(s)
-            nc.gpsimd.tensor_scalar(out=il[:, N_TILE - G_COLS - G_LAP:, :],
-                                    in0=planes[s][:, :, N_TILE - G_COLS - G_LAP:].rearrange("p t n -> p n t"),
+            first = N_TILE - gpsimd_columns(s) - G_LAP
+            nc.gpsimd.tensor_scalar(out=il[:, first:, :],
+                                    in0=planes[s][:, :, first:].rearrange("p t n -> p n t"),
                                     scalar1=1.0, scalar2=0.0, op0=ALU.mult, op1=ALU.add)
 
         def interleave(s):
             il = pair_tile(s)
-            n = N_TILE - G_COLS if s >= G_FROM else N_TILE
+            n = N_TILE - gpsimd_columns(s)
             nc.vector.tensor_copy(out=il[:, 0:n, :].rearrange("p (c i) t -> p c t i", i=4),
                                   in_=planes[s][:, :, 0:n].rearrange("p t (c i) -> p c t i", i=4))
 

@@ -46,7 +46,9 @@ LAG_SCALE = 7
 def vector_planes(s):
     if s < 3:
         return 2
-    if s >= 10 or s == 7:
+    if s == 7:
+        return 0
+    if s >= 10 and s % 5 != 0:
         return 0
     return 1
 
@@ -59,8 +61,8 @@ def gpsimd_columns(s):
     if s < G_FROM:
         return 0
     if s >= LAG_SCALE and vector_scales(s - LAG_SCALE):
-        return 256
-    return 192
+        return 288
+    return 208
 
 
 def tile_attn_pa_kernel(tc, x, W_qk_bytes, W_qk_scale, out_0, out_1):

@@ -48,7 +48,7 @@ def vector_planes(s):
         return 2
     if s == 7:
         return 0
-    if s >= 10 and s % 5 != 0:
+    if s >= 10 and s % 4 != 2:
         return 0
     return 1
 
@@ -61,8 +61,8 @@ def gpsimd_columns(s):
     if s < G_FROM:
         return 0
     if s >= LAG_SCALE and vector_scales(s - LAG_SCALE):
-        return 288
-    return 208
+        return 320
+    return 224
 
 
 def tile_attn_pa_kernel(tc, x, W_qk_bytes, W_qk_scale, out_0, out_1):

@@ -218,8 +218,8 @@ def tile_attn_pa_kernel(tc, x, W_qk_bytes, W_qk_scale, out_0, out_1):
         def interleave_gpsimd(s):
             il = pair_tile(s)
             first = N_TILE - gpsimd_columns(s) - G_LAP
-            nc.gpsimd.tensor_scalar(out=il[:, first:, :],
-                                    in0=planes[s][:, :, first:].rearrange("p t n -> p n t"),
+            nc.gpsimd.tensor_scalar(out=il[:, first:, :].rearrange("p (c i) t -> p c t i", i=4),
+                                    in0=planes[s][:, :, first:].rearrange("p t (c i) -> p c t i", i=4),
                                     scalar1=1.0, scalar2=0.0, op0=ALU.mult, op1=ALU.add)
 
         def interleave(s):

from contextlib import ExitStack
import math

import concourse.mybir as mybir
from concourse.masks import make_identity

F32 = mybir.dt.float32
BF16 = mybir.dt.bfloat16
U32 = mybir.dt.uint32
U8 = mybir.dt.uint8
I32 = mybir.dt.int32
FP8 = mybir.dt.float8_e4m3fn
FP8X4 = mybir.dt.float8_e4m3fn_x4
ALU = mybir.AluOpType
ACT = mybir.ActivationFunctionType

B, T, D, H, DH = 2, 256, 2048, 16, 128
E = H * DH
EPS = 1e-6
ROPE_BASE = 10000.0
FLOPS = 2 * B * T * D * 2 * E

P = 128
PACK = 4
K_PASS = P * PACK
PASSES = D // K_PASS
N_TILE = 512
CHUNKS = 2 * E // N_TILE
HEADS_PER_CHUNK = N_TILE // DH
M_TILES = B * T // P
HALF = DH // 2
STEPS = CHUNKS * PASSES
EPI_LAG = 5

TOK = B * T
HEADS = 2 * H
LAG_MX = 4
LAG_ROT = 5
LAG_NORM = 6
PIN_FROM = 5
G_LAP = 4
G_FROM = 5
LAG_SCALE = 7


def vector_planes(s):
    if s < 3:
        return 2
    if s == 7:
        return 0
    if s >= 10 and s % 4 != 2:
        return 0
    return 1


def vector_scales(hd):
    return hd < 21 or hd >= 28


def gpsimd_columns(s):
    if s < G_FROM:
        return 0
    if s >= LAG_SCALE and vector_scales(s - LAG_SCALE):
        return 320
    return 224


def tile_attn_pa_kernel(tc, x, W_qk_bytes, W_qk_scale, out_0, out_1):
    nc = tc.nc
    outs = (out_0, out_1)
    xv = x.flatten_outer_dims().rearrange("(m p) k -> p m k", p=P)
    wv = W_qk_bytes.rearrange("(g p t) n -> g p t n", p=P, t=PACK)

    with ExitStack() as ctx:
        const = ctx.enter_context(tc.tile_pool(name="const", bufs=1))
        xpool = ctx.enter_context(tc.tile_pool(name="xpool", bufs=1))
        wbytes = ctx.enter_context(tc.tile_pool(name="wbytes", bufs=STEPS))
        wprep = ctx.enter_context(tc.tile_pool(name="wprep", bufs=3))
        wq = ctx.enter_context(tc.tile_pool(name="wq", bufs=12))
        epi = ctx.enter_context(tc.tile_pool(name="epi", bufs=4))
        small = ctx.enter_context(tc.tile_pool(name="small", bufs=6))
        psum = ctx.enter_context(tc.psum_pool(name="psum", bufs=4))

        sc = const.tile([P, PASSES * PACK], F32, name="sc")
        nc.scalar.dma_start(
            out=sc[:].rearrange("p (g t) -> p g t", t=PACK),
            in_=W_qk_scale.rearrange("(g p t) o -> p g (t o)", p=P, t=PACK),
        )
        wb = []
        xs = []

        def load_w(s):
            c, g = divmod(s, PASSES)
            w_codes_in = wbytes.tile([P, PACK, N_TILE], U8, name="w_codes_in")
            nc.sync.dma_start(out=w_codes_in[:], in_=wv[g][:, :, c * N_TILE:(c + 1) * N_TILE])
            wb.append(w_codes_in)

        def load_x(g):
            x_rows = xpool.tile([P, M_TILES, K_PASS], BF16, name="x_rows%d" % g)
            nc.sync.dma_start(out=x_rows[:], in_=xv[:, :, g * K_PASS:(g + 1) * K_PASS])
            xs.append(x_rows)

        for s in range(3):
            load_w(s)
        for g in range(PASSES):
            load_x(g)
            load_w(g + 3)
        for s in range(PASSES + 3, STEPS):
            load_w(s)

        zero = const.tile([P, 1], F32, name="zero")
        nc.vector.memset(zero[:], 0.0)
        warm = const.tile([P, 1], F32, name="warm")
        nc.scalar.activation(out=warm[:], in_=zero[:], func=ACT.Sin)
        ident = const.tile([P, P], F32, name="ident")
        make_identity(nc, ident[:])
        swp = const.tile([P, P], F32, name="swp")
        nc.vector.tensor_copy(out=swp[:, 0:HALF], in_=ident[:, HALF:P])
        nc.vector.tensor_copy(out=swp[:, HALF:P], in_=ident[:, 0:HALF])
        pos_i = const.tile([P, 2], I32, name="pos_i")
        nc.gpsimd.iota(pos_i[:], pattern=[[P, 2]], base=0, channel_multiplier=1)
        pos = const.tile([P, 2], F32, name="pos")
        nc.vector.tensor_copy(out=pos[:], in_=pos_i[:])
        tau = const.tile([P, HALF], F32, name="tau")
        nc.vector.memset(tau[:, 0:1], 1.0)
        nc.vector.tensor_scalar(out=tau[:, 0:1], in0=tau[:, 0:1], scalar1=1.0 / (2.0 * math.pi),
                                scalar2=None, op0=ALU.mult)
        ratio = ROPE_BASE ** (-1.0 / HALF)
        n = 1
        while n < HALF:
            nc.vector.tensor_scalar(out=tau[:, n:2 * n], in0=tau[:, 0:n], scalar1=ratio ** n,
                                    scalar2=None, op0=ALU.mult)
            n *= 2
        turns = const.tile([P, 2, 2, HALF], F32, name="turns")
        for a in range(2):
            nc.vector.tensor_scalar(out=turns[:, a, 0, :], in0=tau[:], scalar1=pos[:, a:a + 1],
                                    scalar2=None, op0=ALU.mult)
            nc.vector.tensor_scalar(out=turns[:, a, 1, :], in0=tau[:], scalar1=pos[:, a:a + 1],
                                    scalar2=0.25, op0=ALU.mult, op1=ALU.add)
        whole_i = const.tile([P, 2, 2, HALF], I32, name="whole_i")
        nc.vector.tensor_copy(out=whole_i[:], in_=turns[:])
        whole = const.tile([P, 2, 2, HALF], F32, name="whole")
        nc.vector.tensor_copy(out=whole[:], in_=whole_i[:])
        frac = const.tile([P, 2, 2, HALF], F32, name="frac")
        nc.vector.tensor_tensor(out=frac[:], in0=turns[:], in1=whole[:], op=ALU.subtract)
        over = const.tile([P, 2, 2, HALF], F32, name="over")
        nc.vector.tensor_scalar(out=over[:], in0=frac[:], scalar1=0.5, scalar2=None, op0=ALU.is_gt)
        nc.vector.tensor_tensor(out=frac[:], in0=frac[:], in1=over[:], op=ALU.subtract)
        trig = const.tile([P, 2, 4, HALF], F32, name="trig")
        nc.scalar.activation(out=trig[:, :, 0, :], in_=frac[:, :, 0, :], func=ACT.Sin, scale=2.0 * math.pi)
        nc.scalar.activation(out=trig[:, :, 1, :], in_=frac[:, :, 0, :], func=ACT.Sin, scale=-2.0 * math.pi)
        nc.scalar.activation(out=trig[:, :, 2, :], in_=frac[:, :, 1, :], func=ACT.Sin, scale=2.0 * math.pi)
        nc.scalar.activation(out=trig[:, :, 3, :], in_=frac[:, :, 1, :], func=ACT.Sin, scale=2.0 * math.pi)
        eps_col = const.tile([P, 1], F32, name="eps_col")
        nc.vector.memset(eps_col[:], EPS)
        tables = []

        def turn_tables():
            tab_ps = psum.tile([P, 2, 2, P], F32, name="tab_ps", tag="tr")
            for k in range(2):
                for a in range(2):
                    nc.tensor.transpose(tab_ps[:, k, a, :],
                                        trig[:, a, 2 * k:2 * k + 2, :].rearrange("p w i -> p (w i)"), ident[:])
            tab = const.tile([P, 2, T], F32, name="tab")
            nc.vector.tensor_copy(out=tab[:].rearrange("p k (a t) -> p k a t", a=2), in_=tab_ps[:])
            tables.append(tab)
            warm_root = const.tile([P, 1], F32, name="warm_root")
            nc.scalar.activation(out=warm_root[:], in_=trig[:, 1, 3, 0:1], func=ACT.Abs_reciprocal_sqrt, scale=0.0,
                                 bias=eps_col[:, 0:1])

        x_codes = []
        x_scales = []

        def prep_x(g):
            words = xs[g][:].bitcast(F32)
            x_grouped = xpool.tile([P, TOK * PACK], BF16, name="x_grouped%d" % g, align_bytes=64)
            gw = x_grouped[:].bitcast(F32).rearrange("p (m r u) -> p m r u", m=M_TILES, u=2)
            for mp in range(M_TILES // 2):
                xt = psum.tile([P, 2, 2, P], F32, name="xt", tag="tr")
                for mi in range(2):
                    for u in range(2):
                        nc.tensor.transpose(xt[:, mi, u, :], words[:, 2 * mp + mi, u::2], ident[:])
                src = xt[:].rearrange("p m u r -> p m r u")
                dst = gw[:, 2 * mp:2 * mp + 2, :, :]
                nc.scalar.copy(out=dst, in_=src)
            xc = xpool.tile([P, TOK], U32, name="x_codes%d" % g, align_bytes=64)
            xsc = xpool.tile([P, TOK], U8, name="x_scales%d" % g, align_bytes=64)
            nc.vector.quantize_mx(out=xc[:].bitcast(FP8X4), scales=xsc[:], in_=x_grouped[:])
            x_codes.append(xc)
            x_scales.append(xsc)

        planes = {}
        grouped = {}
        w_codes = {}
        w_scales = {}
        acc = {}

        def widen_scalar(s):
            g = s % PASSES
            pl = wprep.tile([P, PACK, N_TILE], BF16, name="pl", bufs=7)
            for t in range(vector_planes(s), PACK):
                nc.scalar.activation(out=pl[:, t, :], in_=wb[s][:, t, :].bitcast(FP8), func=ACT.Copy,
                                     scale=sc[:, g * PACK + t:g * PACK + t + 1])
            planes[s] = pl

        def widen_vector(s):
            g = s % PASSES
            for t in range(vector_planes(s)):
                nc.vector.tensor_scalar(out=planes[s][:, t, :], in0=wb[s][:, t, :].bitcast(FP8),
                                        scalar1=sc[:, g * PACK + t:g * PACK + t + 1], scalar2=None, op0=ALU.mult)

        def pair_tile(s):
            if s not in grouped:
                il = wprep.tile([P, N_TILE, PACK], BF16, name="il", align_bytes=64, bufs=4)
                grouped[s] = il
            return grouped[s]

        def interleave_gpsimd(s):
            il = pair_tile(s)
            first = N_TILE - gpsimd_columns(s) - G_LAP
            nc.gpsimd.tensor_scalar(out=il[:, first:, :].rearrange("p (c i) t -> p c t i", i=4),
                                    in0=planes[s][:, :, first:].rearrange("p t (c i) -> p c t i", i=4),
                                    scalar1=1.0, scalar2=0.0, op0=ALU.mult, op1=ALU.add)

        def interleave(s):
            il = pair_tile(s)
            n = N_TILE - gpsimd_columns(s)
            nc.vector.tensor_copy(out=il[:, 0:n, :].rearrange("p (c i) t -> p c t i", i=4),
                                  in_=planes[s][:, :, 0:n].rearrange("p t (c i) -> p c t i", i=4))

        def quantize(j):
            wc = wq.tile([P, N_TILE], U32, name="wc", align_bytes=64)
            ws = wq.tile([P, N_TILE], U8, name="ws", align_bytes=64)
            nc.vector.quantize_mx(out=wc[:].bitcast(FP8X4), scales=ws[:],
                                  in_=grouped[j][:].rearrange("p n t -> p (n t)"))
            w_codes[j] = wc
            w_scales[j] = ws

        def multiply(hd):
            c, j = divmod(hd, HEADS_PER_CHUNK)
            bank = psum.tile([P, TOK], F32, name="acc", tag="mx")
            for g in range(PASSES):
                s = c * PASSES + g
                cols = slice(j * DH, (j + 1) * DH)
                nc.tensor.matmul_mx(
                    out=bank[:],
                    lhsT=w_codes[s][:, cols].bitcast(FP8X4), lhsT_scale=w_scales[s][:, cols],
                    rhs=x_codes[g][:].bitcast(FP8X4), rhs_scale=x_scales[g][:],
                    start=(g == 0), stop=(g == PASSES - 1),
                )
            acc[hd] = bank

        rot = {}
        turned = {}
        norm = {}
        BOTH = (0, 1)

        def rotate(hd, bs=BOTH):
            toks = slice(bs[0] * T, (bs[-1] + 1) * T)
            shape = [P, 2, len(bs), T]
            prod = epi.tile([P, 2, len(bs) * T], F32, name="prod")
            nc.vector.tensor_tensor(out=prod[:].rearrange("p k (b t) -> p k b t", t=T),
                                    in0=acc[hd][:, toks].rearrange("p (b t) -> p b t", t=T).unsqueeze(1).to_broadcast(shape),
                                    in1=tables[0][:].unsqueeze(2).to_broadcast(shape), op=ALU.mult)
            rot[(hd, bs)] = prod

        def turn(hd, bs=BOTH, tag="tr"):
            prod = rot[(hd, bs)]
            back = psum.tile([P, 2 * len(bs), P], F32, name="back", tag=tag)
            for m in range(2 * len(bs)):
                cols = slice(m * P, (m + 1) * P)
                nc.tensor.matmul(out=back[:, m, :], lhsT=prod[:, 1, cols], rhs=ident[:], is_transpose=True,
                                 start=True, stop=False)
                nc.tensor.matmul(out=back[:, m, :], lhsT=prod[:, 0, cols], rhs=swp[:], is_transpose=True,
                                 start=False, stop=True)
            turned[(hd, bs)] = back

        def epi_norm(hd, bs=BOTH):
            back = turned[(hd, bs)]
            ss = small.tile([P, 2 * len(bs)], F32, name="ss")
            for m in range(2 * len(bs)):
                junk = small.tile([P, DH], F32, name="junk", bufs=2)
                nc.scalar.activation(out=junk[:], in_=back[:, m, :], func=ACT.Square, accum_out=ss[:, m:m + 1])
            r = small.tile([P, 2 * len(bs)], F32, name="r")
            nc.scalar.activation(out=r[:], in_=ss[:], func=ACT.Abs_reciprocal_sqrt, scale=1.0 / DH,
                                 bias=eps_col[:, 0:1])
            norm[(hd, bs)] = r

        def epi_scale_store(hd, bs=BOTH):
            back = turned[(hd, bs)]
            r = norm[(hd, bs)]
            res = epi.tile([P, 2 * len(bs), DH], F32, name="res", bufs=4)
            if vector_scales(hd):
                nc.vector.tensor_tensor(out=res[:], in0=back[:],
                                        in1=r[:].unsqueeze(2).to_broadcast([P, 2 * len(bs), DH]), op=ALU.mult)
            else:
                for m in range(2 * len(bs)):
                    nc.scalar.activation(out=res[:, m, :], in_=back[:, m, :], func=ACT.Copy, scale=r[:, m:m + 1])
            dst = outs[hd // H]
            for k in range(len(bs)):
                nc.sync.dma_start(out=dst[bs[k], hd % H, :, :].rearrange("(a p) d -> p a d", p=P),
                                  in_=res[:, 2 * k:2 * k + 2, :])

        for s in range(3):
            widen_scalar(s)
            widen_vector(s)
        widen_scalar(3)
        def one_round(i):
            if 0 <= i - LAG_NORM < HEADS:
                epi_norm(i - LAG_NORM)
            if i + 4 < STEPS:
                widen_scalar(i + 4)
            if i + 3 < STEPS:
                widen_vector(i + 3)
            if i < STEPS:
                interleave(i)
                if i >= G_FROM:
                    interleave_gpsimd(i)
            if i < PASSES:
                prep_x(i)
            if i == PASSES - 1:
                turn_tables()
            if i >= 1:
                quantize(i - 1)
            if 0 <= i - LAG_MX < HEADS:
                multiply(i - LAG_MX)
            if 0 <= i - LAG_ROT < HEADS:
                rotate(i - LAG_ROT)
            if 0 <= i - LAG_SCALE < HEADS:
                epi_scale_store(i - LAG_SCALE)
            if 0 <= i - LAG_ROT < HEADS:
                turn(i - LAG_ROT)

        for i in range(PIN_FROM):
            one_round(i)
        with tc.manual_schedule(engines={mybir.EngineType.DVE, mybir.EngineType.Pool}):
            for i in range(PIN_FROM, STEPS):
                one_round(i)
        quantize(STEPS - 1)
        for hd in range(STEPS - LAG_MX, HEADS - 1):
            multiply(hd)
        rotate(STEPS - LAG_ROT)
        turn(STEPS - LAG_ROT)
        multiply(HEADS - 1)
        for hd in range(STEPS - LAG_ROT + 1, HEADS + 3):
            if hd - 2 < HEADS:
                epi_norm(hd - 2)
            if hd < HEADS:
                rotate(hd)
                turn(hd)
            epi_scale_store(hd - 3)
